import numpy as np
import ml_dtypes

BF16 = ml_dtypes.bfloat16


def bf(x):
    return np.asarray(x, np.float32).astype(BF16)


def f32(x):
    return np.asarray(x, np.float32)


def f64(x):
    return np.asarray(x).astype(np.float64)


def striped(idx):
    return np.tile(idx.reshape(-1, 16).T, (8, 1))


S, P, D, T, F, N = 1024, 128, 256, 128, 128, 2048


def setup_inputs():
    return {
        "table": bf(np.random.standard_normal((S, P))),
        "wp1": bf(np.random.standard_normal((P, D)) / np.sqrt(P)),
        "bp1": f32(0.1 * np.random.standard_normal((D, 1))),
        "wp2": bf(np.random.standard_normal((D, D)) * np.sqrt(2.0 / D)),
        "bp2": f32(0.1 * np.random.standard_normal((D, 1))),
        "t": f32(np.random.uniform(size=(1, N))),
        "wt1": f32(np.random.standard_normal((T, 1))),
        "bt1": f32(0.1 * np.random.standard_normal((T, 1))),
        "wf1": bf(np.random.standard_normal((D + T, F)) / np.sqrt(D + T)),
        "bf1": f32(0.1 * np.random.standard_normal((F, 1))),
        "offs": striped(np.random.permutation(np.tile(np.arange(S), 2))[:N]),
    }


def reference(table, wp1, bp1, wp2, bp2, t, wt1, bt1, wf1, bf1, offs):
    idx = offs[:16].T.reshape(-1)
    a = np.maximum(f64(wp1).T @ f64(table)[idx].T + f64(bp1), 0.0)
    pe = f64(wp2).T @ a + f64(bp2)
    te = np.maximum(f64(wt1) * f64(t) + f64(bt1), 0.0)
    comb = np.concatenate([pe, te], axis=0)
    return np.maximum(f64(wf1).T @ comb + f64(bf1), 0.0)

@@ -1,0 +1,134 @@
+import concourse.mybir as mybir
+from concourse.masks import make_identity
+
+BF16 = mybir.dt.bfloat16
+F32 = mybir.dt.float32
+U16 = mybir.dt.uint16
+RELU = mybir.ActivationFunctionType.Relu
+NO_FUNCTION = mybir.ActivationFunctionType.Identity
+ADD = mybir.AluOpType.add
+MAX = mybir.AluOpType.max
+
+P = 128
+PERSONS = 1024
+BLOCKS = PERSONS // P
+EMBED = 256
+HALVES = EMBED // P
+N = 2048
+PIECE = 512
+PIECES = N // PIECE
+LIST_COLUMNS = PIECE // 16
+
+FLOPS = 2 * N * (P * EMBED + EMBED * EMBED + (EMBED + P) * P)
+
+
+def piece_columns(j):
+    return slice(j * PIECE, (j + 1) * PIECE)
+
+
+def block_columns(b):
+    return slice(b * P, (b + 1) * P)
+
+
+def load_column(nc, pool, name, source):
+    column = pool.tile([P, 1], F32, name=name)
+    nc.scalar.dma_start(column[:], source)
+    return column
+
+
+def add_bias(nc, turn, result, sums, bias, relu):
+    if turn % 2 == 0:
+        nc.scalar.activation(result, sums, RELU if relu else NO_FUNCTION, bias=bias[:])
+    elif relu:
+        nc.vector.tensor_scalar(result, sums, bias[:], 0.0, ADD, MAX)
+    else:
+        nc.vector.tensor_scalar_add(result, sums, bias[:])
+
+
+def tile_manifoldgnnphysicsode_kernel(
+    tc, table, wp1, bp1, wp2, bp2, t, wt1, bt1, wf1, bf1, offs, out
+):
+    nc = tc.nc
+    with tc.tile_pool(name="held", bufs=1) as held:
+        persons = held.tile([P, BLOCKS, P], BF16, name="persons")
+        nc.sync.dma_start(persons[:], table.rearrange("(b p) k -> p b k", p=P))
+        offsets = held.tile([P, N // 16], U16, name="offsets")
+        nc.sync.dma_start(offsets[:], offs)
+        wp1_sb = held.tile([P, EMBED], BF16, name="wp1_sb")
+        nc.sync.dma_start(wp1_sb[:], wp1)
+        times = held.tile([P, N], F32, name="times")
+        for j in range(PIECES):
+            nc.sync.dma_start(
+                times[:, piece_columns(j)], t[0, piece_columns(j)].partition_broadcast(P)
+            )
+
+        wt1_sb = load_column(nc, held, "wt1_sb", wt1)
+        bt1_sb = load_column(nc, held, "bt1_sb", bt1)
+        bp1_sb = [load_column(nc, held, f"bp1_sb{h}", bp1[block_columns(h), :]) for h in range(HALVES)]
+        wp2_sb = held.tile([P, HALVES, EMBED], BF16, name="wp2_sb")
+        nc.scalar.dma_start(wp2_sb[:], wp2.rearrange("(e p) d -> p e d", p=P))
+        bp2_sb = [load_column(nc, held, f"bp2_sb{h}", bp2[block_columns(h), :]) for h in range(HALVES)]
+        wf1_sb = held.tile([P, HALVES + 1, P], BF16, name="wf1_sb")
+        nc.scalar.dma_start(wf1_sb[:], wf1.rearrange("(r p) f -> p r f", p=P))
+        bf1_sb = load_column(nc, held, "bf1_sb", bf1)
+
+        identity = held.tile([P, P], BF16, name="identity")
+        make_identity(nc, identity[:])
+        window = held.tile([P, PERSONS], BF16, name="window")
+        half_blocks = BLOCKS // 2
+        with tc.psum_pool(name="flip", bufs=1) as flip:
+            for side in range(2):
+                flipped = flip.tile([P, half_blocks * P], BF16, name=f"flipped{side}")
+                for b in range(half_blocks):
+                    nc.tensor.transpose(
+                        flipped[:, block_columns(b)], persons[:, side * half_blocks + b, :], identity[:]
+                    )
+                window_half = window[:, side * half_blocks * P : (side + 1) * half_blocks * P]
+                if side == 0:
+                    nc.vector.tensor_copy(window_half, flipped[:])
+                else:
+                    nc.scalar.copy(window_half, flipped[:])
+
+        a_sb = held.tile([P, HALVES, N], BF16, name="a_sb")
+        pe_sb = held.tile([P, HALVES, N], BF16, name="pe_sb")
+        te_sb = held.tile([P, N], BF16, name="te_sb")
+        out_sb = held.tile([P, N], F32, name="out_sb")
+
+        for j in range(PIECES):
+            nc.scalar.activation(
+                te_sb[:, piece_columns(j)], times[:, piece_columns(j)], RELU, bias=bt1_sb[:], scale=wt1_sb[:]
+            )
+
+        with tc.psum_pool(name="banks", bufs=8) as banks:
+            for j in range(PIECES):
+                for h in range(HALVES):
+                    a_ps = banks.tile([P, PIECE], F32, tag="bank")
+                    picked = window[:].indirect(offsets[:, j * LIST_COLUMNS : (j + 1) * LIST_COLUMNS])
+                    nc.tensor.matmul(a_ps[:], wp1_sb[:, block_columns(h)], picked, start=True, stop=True)
+                    add_bias(nc, h, a_sb[:, h, piece_columns(j)], a_ps[:], bp1_sb[h], relu=True)
+
+            for j in range(PIECES):
+                for d in range(HALVES):
+                    pe_ps = banks.tile([P, PIECE], F32, tag="bank")
+                    for e in range(HALVES):
+                        nc.tensor.matmul(
+                            pe_ps[:],
+                            wp2_sb[:, e, block_columns(d)],
+                            a_sb[:, e, piece_columns(j)],
+                            start=(e == 0),
+                            stop=(e == HALVES - 1),
+                        )
+                    add_bias(nc, d, pe_sb[:, d, piece_columns(j)], pe_ps[:], bp2_sb[d], relu=False)
+
+                out_ps = banks.tile([P, PIECE], F32, tag="bank")
+                nc.tensor.matmul(out_ps[:], wf1_sb[:, HALVES, :], te_sb[:, piece_columns(j)], start=True, stop=False)
+                for d in range(HALVES):
+                    nc.tensor.matmul(
+                        out_ps[:],
+                        wf1_sb[:, d, :],
+                        pe_sb[:, d, piece_columns(j)],
+                        start=False,
+                        stop=(d == HALVES - 1),
+                    )
+                add_bias(nc, j, out_sb[:, piece_columns(j)], out_ps[:], bf1_sb, relu=True)
+                nc.sync.dma_start(out[:, piece_columns(j)], out_sb[:, piece_columns(j)])

@@ -12,6 +12,8 @@ MAX = mybir.AluOpType.max
 P = 128
 PERSONS = 1024
 BLOCKS = PERSONS // P
+CHUNKS = 4
+CHUNK_BLOCKS = BLOCKS // CHUNKS
 EMBED = 256
 HALVES = EMBED // P
 N = 2048
@@ -50,21 +52,27 @@ def tile_manifoldgnnphysicsode_kernel(
 ):
     nc = tc.nc
     with tc.tile_pool(name="held", bufs=1) as held:
-        persons = held.tile([P, BLOCKS, P], BF16, name="persons")
-        nc.sync.dma_start(persons[:], table.rearrange("(b p) k -> p b k", p=P))
+        persons = []
+        table_blocks = table.rearrange("(b p) k -> p b k", p=P)
+        for c in range(CHUNKS):
+            chunk = held.tile([P, CHUNK_BLOCKS, P], BF16, name=f"persons{c}")
+            queue = nc.sync if c % 2 == 0 else nc.scalar
+            queue.dma_start(chunk[:], table_blocks[:, c * CHUNK_BLOCKS : (c + 1) * CHUNK_BLOCKS, :])
+            persons.append(chunk)
+
         offsets = held.tile([P, N // 16], U16, name="offsets")
         nc.sync.dma_start(offsets[:], offs)
-        wp1_sb = held.tile([P, EMBED], BF16, name="wp1_sb")
-        nc.sync.dma_start(wp1_sb[:], wp1)
         times = held.tile([P, N], F32, name="times")
         for j in range(PIECES):
             nc.sync.dma_start(
                 times[:, piece_columns(j)], t[0, piece_columns(j)].partition_broadcast(P)
             )
 
+        wp1_sb = held.tile([P, EMBED], BF16, name="wp1_sb")
+        nc.scalar.dma_start(wp1_sb[:], wp1)
+        bp1_sb = [load_column(nc, held, f"bp1_sb{h}", bp1[block_columns(h), :]) for h in range(HALVES)]
         wt1_sb = load_column(nc, held, "wt1_sb", wt1)
         bt1_sb = load_column(nc, held, "bt1_sb", bt1)
-        bp1_sb = [load_column(nc, held, f"bp1_sb{h}", bp1[block_columns(h), :]) for h in range(HALVES)]
         wp2_sb = held.tile([P, HALVES, EMBED], BF16, name="wp2_sb")
         nc.scalar.dma_start(wp2_sb[:], wp2.rearrange("(e p) d -> p e d", p=P))
         bp2_sb = [load_column(nc, held, f"bp2_sb{h}", bp2[block_columns(h), :]) for h in range(HALVES)]
@@ -72,22 +80,21 @@ def tile_manifoldgnnphysicsode_kernel(
         nc.scalar.dma_start(wf1_sb[:], wf1.rearrange("(r p) f -> p r f", p=P))
         bf1_sb = load_column(nc, held, "bf1_sb", bf1)
 
+        zero = held.tile([P, 1], F32, name="zero")
+        nc.vector.memset(zero[:], 0.0)
+        unused = held.tile([P, 1], F32, name="unused")
+        nc.scalar.activation(unused[:], zero[:], RELU)
+
         identity = held.tile([P, P], BF16, name="identity")
         make_identity(nc, identity[:])
         window = held.tile([P, PERSONS], BF16, name="window")
-        half_blocks = BLOCKS // 2
         with tc.psum_pool(name="flip", bufs=1) as flip:
-            for side in range(2):
-                flipped = flip.tile([P, half_blocks * P], BF16, name=f"flipped{side}")
-                for b in range(half_blocks):
-                    nc.tensor.transpose(
-                        flipped[:, block_columns(b)], persons[:, side * half_blocks + b, :], identity[:]
-                    )
-                window_half = window[:, side * half_blocks * P : (side + 1) * half_blocks * P]
-                if side == 0:
-                    nc.vector.tensor_copy(window_half, flipped[:])
-                else:
-                    nc.scalar.copy(window_half, flipped[:])
+            for c in range(CHUNKS):
+                flipped = flip.tile([P, CHUNK_BLOCKS * P], BF16, name=f"flipped{c}")
+                for b in range(CHUNK_BLOCKS):
+                    nc.tensor.transpose(flipped[:, block_columns(b)], persons[c][:, b, :], identity[:])
+                window_chunk = window[:, c * CHUNK_BLOCKS * P : (c + 1) * CHUNK_BLOCKS * P]
+                nc.vector.tensor_copy(window_chunk, flipped[:])
 
         a_sb = held.tile([P, HALVES, N], BF16, name="a_sb")
         pe_sb = held.tile([P, HALVES, N], BF16, name="pe_sb")

@@ -32,19 +32,21 @@ def block_columns(b):
     return slice(b * P, (b + 1) * P)
 
 
-def load_column(nc, pool, name, source):
-    column = pool.tile([P, 1], F32, name=name)
-    nc.scalar.dma_start(column[:], source)
-    return column
+def load_columns(nc, queue, pool, name, vector):
+    blocks = vector.shape[0] // P
+    columns = pool.tile([P, blocks], F32, name=name)
+    with nc.allow_non_contiguous_dma(reason="a small vector, one element to a partition"):
+        queue.dma_start(columns[:], vector.rearrange("(b p) one -> p (b one)", p=P))
+    return columns
 
 
 def add_bias(nc, turn, result, sums, bias, relu):
     if turn % 2 == 0:
-        nc.scalar.activation(result, sums, RELU if relu else NO_FUNCTION, bias=bias[:])
+        nc.scalar.activation(result, sums, RELU if relu else NO_FUNCTION, bias=bias)
     elif relu:
-        nc.vector.tensor_scalar(result, sums, bias[:], 0.0, ADD, MAX)
+        nc.vector.tensor_scalar(result, sums, bias, 0.0, ADD, MAX)
     else:
-        nc.vector.tensor_scalar_add(result, sums, bias[:])
+        nc.vector.tensor_scalar_add(result, sums, bias)
 
 
 def tile_manifoldgnnphysicsode_kernel(
@@ -52,6 +54,10 @@ def tile_manifoldgnnphysicsode_kernel(
 ):
     nc = tc.nc
     with tc.tile_pool(name="held", bufs=1) as held:
+        identity = held.tile([P, P], BF16, name="identity")
+        make_identity(nc, identity[:])
+
+
         persons = []
         table_blocks = table.rearrange("(b p) k -> p b k", p=P)
         for c in range(CHUNKS):
@@ -59,34 +65,29 @@ def tile_manifoldgnnphysicsode_kernel(
             queue = nc.sync if c % 2 == 0 else nc.scalar
             queue.dma_start(chunk[:], table_blocks[:, c * CHUNK_BLOCKS : (c + 1) * CHUNK_BLOCKS, :])
             persons.append(chunk)
-
         offsets = held.tile([P, N // 16], U16, name="offsets")
         nc.sync.dma_start(offsets[:], offs)
-        times = held.tile([P, N], F32, name="times")
-        for j in range(PIECES):
-            nc.sync.dma_start(
-                times[:, piece_columns(j)], t[0, piece_columns(j)].partition_broadcast(P)
-            )
-
         wp1_sb = held.tile([P, EMBED], BF16, name="wp1_sb")
         nc.scalar.dma_start(wp1_sb[:], wp1)
-        bp1_sb = [load_column(nc, held, f"bp1_sb{h}", bp1[block_columns(h), :]) for h in range(HALVES)]
-        wt1_sb = load_column(nc, held, "wt1_sb", wt1)
-        bt1_sb = load_column(nc, held, "bt1_sb", bt1)
+        bp1_sb = load_columns(nc, nc.scalar, held, "bp1_sb", bp1)
+        times = held.tile([P, N], F32, name="times")
+        nc.sync.dma_start(times[:], t[0, :].partition_broadcast(P))
+
+        wt1_sb = load_columns(nc, nc.gpsimd, held, "wt1_sb", wt1)
+        bt1_sb = load_columns(nc, nc.gpsimd, held, "bt1_sb", bt1)
+
         wp2_sb = held.tile([P, HALVES, EMBED], BF16, name="wp2_sb")
-        nc.scalar.dma_start(wp2_sb[:], wp2.rearrange("(e p) d -> p e d", p=P))
-        bp2_sb = [load_column(nc, held, f"bp2_sb{h}", bp2[block_columns(h), :]) for h in range(HALVES)]
+        nc.sync.dma_start(wp2_sb[:], wp2.rearrange("(e p) d -> p e d", p=P))
+        bp2_sb = load_columns(nc, nc.sync, held, "bp2_sb", bp2)
         wf1_sb = held.tile([P, HALVES + 1, P], BF16, name="wf1_sb")
-        nc.scalar.dma_start(wf1_sb[:], wf1.rearrange("(r p) f -> p r f", p=P))
-        bf1_sb = load_column(nc, held, "bf1_sb", bf1)
+        nc.sync.dma_start(wf1_sb[:], wf1.rearrange("(r p) f -> p r f", p=P))
+        bf1_sb = load_columns(nc, nc.sync, held, "bf1_sb", bf1)
 
         zero = held.tile([P, 1], F32, name="zero")
         nc.vector.memset(zero[:], 0.0)
         unused = held.tile([P, 1], F32, name="unused")
         nc.scalar.activation(unused[:], zero[:], RELU)
 
-        identity = held.tile([P, P], BF16, name="identity")
-        make_identity(nc, identity[:])
         window = held.tile([P, PERSONS], BF16, name="window")
         with tc.psum_pool(name="flip", bufs=1) as flip:
             for c in range(CHUNKS):
@@ -112,7 +113,7 @@ def tile_manifoldgnnphysicsode_kernel(
                     a_ps = banks.tile([P, PIECE], F32, tag="bank")
                     picked = window[:].indirect(offsets[:, j * LIST_COLUMNS : (j + 1) * LIST_COLUMNS])
                     nc.tensor.matmul(a_ps[:], wp1_sb[:, block_columns(h)], picked, start=True, stop=True)
-                    add_bias(nc, h, a_sb[:, h, piece_columns(j)], a_ps[:], bp1_sb[h], relu=True)
+                    add_bias(nc, h, a_sb[:, h, piece_columns(j)], a_ps[:], bp1_sb[:, h : h + 1], relu=True)
 
             for j in range(PIECES):
                 for d in range(HALVES):
@@ -125,7 +126,7 @@ def tile_manifoldgnnphysicsode_kernel(
                             start=(e == 0),
                             stop=(e == HALVES - 1),
                         )
-                    add_bias(nc, d, pe_sb[:, d, piece_columns(j)], pe_ps[:], bp2_sb[d], relu=False)
+                    add_bias(nc, d, pe_sb[:, d, piece_columns(j)], pe_ps[:], bp2_sb[:, d : d + 1], relu=False)
 
                 out_ps = banks.tile([P, PIECE], F32, tag="bank")
                 nc.tensor.matmul(out_ps[:], wf1_sb[:, HALVES, :], te_sb[:, piece_columns(j)], start=True, stop=False)
@@ -137,5 +138,5 @@ def tile_manifoldgnnphysicsode_kernel(
                         start=False,
                         stop=(d == HALVES - 1),
                     )
-                add_bias(nc, j, out_sb[:, piece_columns(j)], out_ps[:], bf1_sb, relu=True)
+                add_bias(nc, j, out_sb[:, piece_columns(j)], out_ps[:], bf1_sb[:], relu=True)
                 nc.sync.dma_start(out[:, piece_columns(j)], out_sb[:, piece_columns(j)])

@@ -20,6 +20,7 @@ N = 2048
 PIECE = 512
 PIECES = N // PIECE
 LIST_COLUMNS = PIECE // 16
+WARMING_MATMULS = 4
 
 FLOPS = 2 * N * (P * EMBED + EMBED * EMBED + (EMBED + P) * P)
 
@@ -90,6 +91,12 @@ def tile_manifoldgnnphysicsode_kernel(
 
         window = held.tile([P, PERSONS], BF16, name="window")
         with tc.psum_pool(name="flip", bufs=1) as flip:
+            zeros = held.tile([P, PIECE], BF16, name="zeros")
+            nc.vector.memset(zeros[:], 0.0)
+            unread_ps = flip.tile([P, PIECE], F32, name="unread_ps")
+            for i in range(WARMING_MATMULS):
+                nc.tensor.matmul(unread_ps[:], zeros[:, block_columns(0)], zeros[:], start=True, stop=True)
+
             for c in range(CHUNKS):
                 flipped = flip.tile([P, CHUNK_BLOCKS * P], BF16, name=f"flipped{c}")
                 for b in range(CHUNK_BLOCKS):

@@ -19,8 +19,8 @@ HALVES = EMBED // P
 N = 2048
 PIECE = 512
 PIECES = N // PIECE
+HALF_PIECE = PIECE // 2
 LIST_COLUMNS = PIECE // 16
-WARMING_MATMULS = 4
 
 FLOPS = 2 * N * (P * EMBED + EMBED * EMBED + (EMBED + P) * P)
 
@@ -91,12 +91,6 @@ def tile_manifoldgnnphysicsode_kernel(
 
         window = held.tile([P, PERSONS], BF16, name="window")
         with tc.psum_pool(name="flip", bufs=1) as flip:
-            zeros = held.tile([P, PIECE], BF16, name="zeros")
-            nc.vector.memset(zeros[:], 0.0)
-            unread_ps = flip.tile([P, PIECE], F32, name="unread_ps")
-            for i in range(WARMING_MATMULS):
-                nc.tensor.matmul(unread_ps[:], zeros[:, block_columns(0)], zeros[:], start=True, stop=True)
-
             for c in range(CHUNKS):
                 flipped = flip.tile([P, CHUNK_BLOCKS * P], BF16, name=f"flipped{c}")
                 for b in range(CHUNK_BLOCKS):
@@ -122,7 +116,7 @@ def tile_manifoldgnnphysicsode_kernel(
                     nc.tensor.matmul(a_ps[:], wp1_sb[:, block_columns(h)], picked, start=True, stop=True)
                     add_bias(nc, h, a_sb[:, h, piece_columns(j)], a_ps[:], bp1_sb[:, h : h + 1], relu=True)
 
-            for j in range(PIECES):
+            def second_layer(j):
                 for d in range(HALVES):
                     pe_ps = banks.tile([P, PIECE], F32, tag="bank")
                     for e in range(HALVES):
@@ -135,15 +129,21 @@ def tile_manifoldgnnphysicsode_kernel(
                         )
                     add_bias(nc, d, pe_sb[:, d, piece_columns(j)], pe_ps[:], bp2_sb[:, d : d + 1], relu=False)
 
-                out_ps = banks.tile([P, PIECE], F32, tag="bank")
-                nc.tensor.matmul(out_ps[:], wf1_sb[:, HALVES, :], te_sb[:, piece_columns(j)], start=True, stop=False)
-                for d in range(HALVES):
-                    nc.tensor.matmul(
-                        out_ps[:],
-                        wf1_sb[:, d, :],
-                        pe_sb[:, d, piece_columns(j)],
-                        start=False,
-                        stop=(d == HALVES - 1),
-                    )
-                add_bias(nc, j, out_sb[:, piece_columns(j)], out_ps[:], bf1_sb[:], relu=True)
-                nc.sync.dma_start(out[:, piece_columns(j)], out_sb[:, piece_columns(j)])
+            def flow_layer(j):
+                for side in range(2):
+                    first = j * PIECE + side * HALF_PIECE
+                    columns = slice(first, first + HALF_PIECE)
+                    out_ps = banks.tile([P, HALF_PIECE], F32, tag="bank")
+                    nc.tensor.matmul(out_ps[:], wf1_sb[:, HALVES, :], te_sb[:, columns], start=True, stop=False)
+                    for d in range(HALVES):
+                        nc.tensor.matmul(
+                            out_ps[:], wf1_sb[:, d, :], pe_sb[:, d, columns], start=False, stop=(d == HALVES - 1)
+                        )
+                    add_bias(nc, side, out_sb[:, columns], out_ps[:], bf1_sb[:], relu=True)
+                    nc.sync.dma_start(out[:, columns], out_sb[:, columns])
+
+            second_layer(0)
+            for j in range(1, PIECES):
+                second_layer(j)
+                flow_layer(j - 1)
+            flow_layer(PIECES - 1)

@@ -21,6 +21,7 @@ PIECE = 512
 PIECES = N // PIECE
 HALF_PIECE = PIECE // 2
 LIST_COLUMNS = PIECE // 16
+WARMING_MATMULS = 3
 
 FLOPS = 2 * N * (P * EMBED + EMBED * EMBED + (EMBED + P) * P)
 
@@ -55,6 +56,9 @@ def tile_manifoldgnnphysicsode_kernel(
 ):
     nc = tc.nc
     with tc.tile_pool(name="held", bufs=1) as held:
+        zeros = held.tile([P, PIECE], BF16, name="zeros")
+        nc.vector.memset(zeros[:], 0.0)
+
         identity = held.tile([P, P], BF16, name="identity")
         make_identity(nc, identity[:])
 
@@ -91,6 +95,10 @@ def tile_manifoldgnnphysicsode_kernel(
 
         window = held.tile([P, PERSONS], BF16, name="window")
         with tc.psum_pool(name="flip", bufs=1) as flip:
+            unread_ps = flip.tile([P, PIECE], F32, name="unread_ps")
+            for i in range(WARMING_MATMULS):
+                nc.tensor.matmul(unread_ps[:], zeros[:, block_columns(0)], zeros[:], start=True, stop=True)
+
             for c in range(CHUNKS):
                 flipped = flip.tile([P, CHUNK_BLOCKS * P], BF16, name=f"flipped{c}")
                 for b in range(CHUNK_BLOCKS):

@@ -75,8 +75,6 @@ def tile_manifoldgnnphysicsode_kernel(
         wp1_sb = held.tile([P, EMBED], BF16, name="wp1_sb")
         nc.scalar.dma_start(wp1_sb[:], wp1)
         bp1_sb = load_columns(nc, nc.scalar, held, "bp1_sb", bp1)
-        times = held.tile([P, N], F32, name="times")
-        nc.sync.dma_start(times[:], t[0, :].partition_broadcast(P))
 
         wt1_sb = load_columns(nc, nc.gpsimd, held, "wt1_sb", wt1)
         bt1_sb = load_columns(nc, nc.gpsimd, held, "bt1_sb", bt1)
@@ -87,6 +85,10 @@ def tile_manifoldgnnphysicsode_kernel(
         wf1_sb = held.tile([P, HALVES + 1, P], BF16, name="wf1_sb")
         nc.sync.dma_start(wf1_sb[:], wf1.rearrange("(r p) f -> p r f", p=P))
         bf1_sb = load_columns(nc, nc.sync, held, "bf1_sb", bf1)
+
+        times = held.tile([P, N], F32, name="times")
+        for j in range(PIECES):
+            nc.sync.dma_start(times[:, piece_columns(j)], t[0, piece_columns(j)].partition_broadcast(P))
 
         zero = held.tile([P, 1], F32, name="zero")
         nc.vector.memset(zero[:], 0.0)

@@ -87,8 +87,7 @@ def tile_manifoldgnnphysicsode_kernel(
         bf1_sb = load_columns(nc, nc.sync, held, "bf1_sb", bf1)
 
         times = held.tile([P, N], F32, name="times")
-        for j in range(PIECES):
-            nc.sync.dma_start(times[:, piece_columns(j)], t[0, piece_columns(j)].partition_broadcast(P))
+        nc.sync.dma_start(times[:], t[0, :].partition_broadcast(P))
 
         zero = held.tile([P, 1], F32, name="zero")
         nc.vector.memset(zero[:], 0.0)

@@ -55,7 +55,7 @@ def tile_manifoldgnnphysicsode_kernel(
     tc, table, wp1, bp1, wp2, bp2, t, wt1, bt1, wf1, bf1, offs, out
 ):
     nc = tc.nc
-    with tc.tile_pool(name="held", bufs=1) as held:
+    with tc.tile_pool(name="held", bufs=1) as held, tc.tile_pool(name="shared", bufs=1) as shared:
         zeros = held.tile([P, PIECE], BF16, name="zeros")
         nc.vector.memset(zeros[:], 0.0)
 
@@ -94,7 +94,8 @@ def tile_manifoldgnnphysicsode_kernel(
         unused = held.tile([P, 1], F32, name="unused")
         nc.scalar.activation(unused[:], zero[:], RELU)
 
-        window = held.tile([P, PERSONS], BF16, name="window")
+        window_tile = shared.tile([P, N], BF16, tag="window_then_te", name="window_tile")
+        window = window_tile[:, :PERSONS]
         with tc.psum_pool(name="flip", bufs=1) as flip:
             unread_ps = flip.tile([P, PIECE], F32, name="unread_ps")
             for i in range(WARMING_MATMULS):
@@ -109,21 +110,21 @@ def tile_manifoldgnnphysicsode_kernel(
 
         a_sb = held.tile([P, HALVES, N], BF16, name="a_sb")
         pe_sb = held.tile([P, HALVES, N], BF16, name="pe_sb")
-        te_sb = held.tile([P, N], BF16, name="te_sb")
         out_sb = held.tile([P, N], F32, name="out_sb")
-
-        for j in range(PIECES):
-            nc.scalar.activation(
-                te_sb[:, piece_columns(j)], times[:, piece_columns(j)], RELU, bias=bt1_sb[:], scale=wt1_sb[:]
-            )
 
         with tc.psum_pool(name="banks", bufs=8) as banks:
             for j in range(PIECES):
                 for h in range(HALVES):
                     a_ps = banks.tile([P, PIECE], F32, tag="bank")
-                    picked = window[:].indirect(offsets[:, j * LIST_COLUMNS : (j + 1) * LIST_COLUMNS])
+                    picked = window.indirect(offsets[:, j * LIST_COLUMNS : (j + 1) * LIST_COLUMNS])
                     nc.tensor.matmul(a_ps[:], wp1_sb[:, block_columns(h)], picked, start=True, stop=True)
                     add_bias(nc, h, a_sb[:, h, piece_columns(j)], a_ps[:], bp1_sb[:, h : h + 1], relu=True)
+
+            te_sb = shared.tile([P, N], BF16, tag="window_then_te", name="te_sb")
+            for j in range(PIECES):
+                nc.scalar.activation(
+                    te_sb[:, piece_columns(j)], times[:, piece_columns(j)], RELU, bias=bt1_sb[:], scale=wt1_sb[:]
+                )
 
             def second_layer(j):
                 for d in range(HALVES):

@@ -76,15 +76,15 @@ def tile_manifoldgnnphysicsode_kernel(
         nc.scalar.dma_start(wp1_sb[:], wp1)
         bp1_sb = load_columns(nc, nc.scalar, held, "bp1_sb", bp1)
 
-        wt1_sb = load_columns(nc, nc.gpsimd, held, "wt1_sb", wt1)
-        bt1_sb = load_columns(nc, nc.gpsimd, held, "bt1_sb", bt1)
-
         wp2_sb = held.tile([P, HALVES, EMBED], BF16, name="wp2_sb")
         nc.sync.dma_start(wp2_sb[:], wp2.rearrange("(e p) d -> p e d", p=P))
         bp2_sb = load_columns(nc, nc.sync, held, "bp2_sb", bp2)
         wf1_sb = held.tile([P, HALVES + 1, P], BF16, name="wf1_sb")
         nc.sync.dma_start(wf1_sb[:], wf1.rearrange("(r p) f -> p r f", p=P))
         bf1_sb = load_columns(nc, nc.sync, held, "bf1_sb", bf1)
+
+        wt1_sb = load_columns(nc, nc.sync, held, "wt1_sb", wt1)
+        bt1_sb = load_columns(nc, nc.sync, held, "bt1_sb", bt1)
 
         times = held.tile([P, N], F32, name="times")
         nc.sync.dma_start(times[:], t[0, :].partition_broadcast(P))

@@ -67,14 +67,13 @@ def tile_manifoldgnnphysicsode_kernel(
         table_blocks = table.rearrange("(b p) k -> p b k", p=P)
         for c in range(CHUNKS):
             chunk = held.tile([P, CHUNK_BLOCKS, P], BF16, name=f"persons{c}")
-            queue = nc.sync if c % 2 == 0 else nc.scalar
-            queue.dma_start(chunk[:], table_blocks[:, c * CHUNK_BLOCKS : (c + 1) * CHUNK_BLOCKS, :])
+            nc.sync.dma_start(chunk[:], table_blocks[:, c * CHUNK_BLOCKS : (c + 1) * CHUNK_BLOCKS, :])
             persons.append(chunk)
         offsets = held.tile([P, N // 16], U16, name="offsets")
         nc.sync.dma_start(offsets[:], offs)
         wp1_sb = held.tile([P, EMBED], BF16, name="wp1_sb")
-        nc.scalar.dma_start(wp1_sb[:], wp1)
-        bp1_sb = load_columns(nc, nc.scalar, held, "bp1_sb", bp1)
+        nc.sync.dma_start(wp1_sb[:], wp1)
+        bp1_sb = load_columns(nc, nc.sync, held, "bp1_sb", bp1)
 
         wp2_sb = held.tile([P, HALVES, EMBED], BF16, name="wp2_sb")
         nc.sync.dma_start(wp2_sb[:], wp2.rearrange("(e p) d -> p e d", p=P))

@@ -21,7 +21,7 @@ PIECE = 512
 PIECES = N // PIECE
 HALF_PIECE = PIECE // 2
 LIST_COLUMNS = PIECE // 16
-WARMING_MATMULS = 3
+WARMING_MATMULS = 10
 
 FLOPS = 2 * N * (P * EMBED + EMBED * EMBED + (EMBED + P) * P)
 
@@ -56,7 +56,7 @@ def tile_manifoldgnnphysicsode_kernel(
 ):
     nc = tc.nc
     with tc.tile_pool(name="held", bufs=1) as held, tc.tile_pool(name="shared", bufs=1) as shared:
-        zeros = held.tile([P, PIECE], BF16, name="zeros")
+        zeros = held.tile([P, P], BF16, name="zeros")
         nc.vector.memset(zeros[:], 0.0)
 
         identity = held.tile([P, P], BF16, name="identity")
@@ -96,9 +96,9 @@ def tile_manifoldgnnphysicsode_kernel(
         window_tile = shared.tile([P, N], BF16, tag="window_then_te", name="window_tile")
         window = window_tile[:, :PERSONS]
         with tc.psum_pool(name="flip", bufs=1) as flip:
-            unread_ps = flip.tile([P, PIECE], F32, name="unread_ps")
+            unread_ps = flip.tile([P, P], F32, name="unread_ps")
             for i in range(WARMING_MATMULS):
-                nc.tensor.matmul(unread_ps[:], zeros[:, block_columns(0)], zeros[:], start=True, stop=True)
+                nc.tensor.matmul(unread_ps[:], zeros[:], zeros[:], start=True, stop=True)
 
             for c in range(CHUNKS):
                 flipped = flip.tile([P, CHUNK_BLOCKS * P], BF16, name=f"flipped{c}")

@@ -14,6 +14,8 @@ PERSONS = 1024
 BLOCKS = PERSONS // P
 CHUNKS = 4
 CHUNK_BLOCKS = BLOCKS // CHUNKS
+CHUNK_ROWS = CHUNK_BLOCKS * P
+PAIRED_CHUNKS = CHUNKS // 2
 EMBED = 256
 HALVES = EMBED // P
 N = 2048
@@ -64,10 +66,13 @@ def tile_manifoldgnnphysicsode_kernel(
 
 
         persons = []
-        table_blocks = table.rearrange("(b p) k -> p b k", p=P)
         for c in range(CHUNKS):
+            rows = table[c * CHUNK_ROWS : (c + 1) * CHUNK_ROWS, :]
             chunk = held.tile([P, CHUNK_BLOCKS, P], BF16, name=f"persons{c}")
-            nc.sync.dma_start(chunk[:], table_blocks[:, c * CHUNK_BLOCKS : (c + 1) * CHUNK_BLOCKS, :])
+            if c < PAIRED_CHUNKS:
+                nc.sync.dma_start(chunk[:], rows.rearrange("(p b) k -> p b k", p=P))
+            else:
+                nc.sync.dma_start(chunk[:], rows.rearrange("(b p) k -> p b k", p=P))
             persons.append(chunk)
         offsets = held.tile([P, N // 16], U16, name="offsets")
         nc.sync.dma_start(offsets[:], offs)
@@ -101,11 +106,16 @@ def tile_manifoldgnnphysicsode_kernel(
                 nc.tensor.matmul(unread_ps[:], zeros[:], zeros[:], start=True, stop=True)
 
             for c in range(CHUNKS):
-                flipped = flip.tile([P, CHUNK_BLOCKS * P], BF16, name=f"flipped{c}")
+                flipped = flip.tile([P, CHUNK_BLOCKS, P], BF16, name=f"flipped{c}")
                 for b in range(CHUNK_BLOCKS):
-                    nc.tensor.transpose(flipped[:, block_columns(b)], persons[c][:, b, :], identity[:])
-                window_chunk = window[:, c * CHUNK_BLOCKS * P : (c + 1) * CHUNK_BLOCKS * P]
-                nc.vector.tensor_copy(window_chunk, flipped[:])
+                    nc.tensor.transpose(flipped[:, b, :], persons[c][:, b, :], identity[:])
+                window_chunk = window[:, c * CHUNK_ROWS : (c + 1) * CHUNK_ROWS]
+                if c < PAIRED_CHUNKS:
+                    nc.vector.tensor_copy(
+                        window_chunk.rearrange("k (p b) -> k p b", p=P), flipped[:].rearrange("k b p -> k p b")
+                    )
+                else:
+                    nc.vector.tensor_copy(window_chunk, flipped[:].rearrange("k b p -> k (b p)"))
 
         a_sb = held.tile([P, HALVES, N], BF16, name="a_sb")
         pe_sb = held.tile([P, HALVES, N], BF16, name="pe_sb")

import concourse.mybir as mybir
from concourse.masks import make_identity

BF16 = mybir.dt.bfloat16
F32 = mybir.dt.float32
U16 = mybir.dt.uint16
RELU = mybir.ActivationFunctionType.Relu
NO_FUNCTION = mybir.ActivationFunctionType.Identity
ADD = mybir.AluOpType.add
MAX = mybir.AluOpType.max

P = 128
PERSONS = 1024
BLOCKS = PERSONS // P
CHUNKS = 4
CHUNK_BLOCKS = BLOCKS // CHUNKS
CHUNK_ROWS = CHUNK_BLOCKS * P
PAIRED_CHUNKS = CHUNKS // 2
EMBED = 256
HALVES = EMBED // P
N = 2048
PIECE = 512
PIECES = N // PIECE
HALF_PIECE = PIECE // 2
LIST_COLUMNS = PIECE // 16
WARMING_MATMULS = 10

FLOPS = 2 * N * (P * EMBED + EMBED * EMBED + (EMBED + P) * P)


def piece_columns(j):
    return slice(j * PIECE, (j + 1) * PIECE)


def block_columns(b):
    return slice(b * P, (b + 1) * P)


def load_columns(nc, queue, pool, name, vector):
    blocks = vector.shape[0] // P
    columns = pool.tile([P, blocks], F32, name=name)
    with nc.allow_non_contiguous_dma(reason="a small vector, one element to a partition"):
        queue.dma_start(columns[:], vector.rearrange("(b p) one -> p (b one)", p=P))
    return columns


def add_bias(nc, turn, result, sums, bias, relu):
    if turn % 2 == 0:
        nc.scalar.activation(result, sums, RELU if relu else NO_FUNCTION, bias=bias)
    elif relu:
        nc.vector.tensor_scalar(result, sums, bias, 0.0, ADD, MAX)
    else:
        nc.vector.tensor_scalar_add(result, sums, bias)


def tile_manifoldgnnphysicsode_kernel(
    tc, table, wp1, bp1, wp2, bp2, t, wt1, bt1, wf1, bf1, offs, out
):
    nc = tc.nc
    with tc.tile_pool(name="held", bufs=1) as held, tc.tile_pool(name="shared", bufs=1) as shared:
        zeros = held.tile([P, P], BF16, name="zeros")
        nc.vector.memset(zeros[:], 0.0)

        identity = held.tile([P, P], BF16, name="identity")
        make_identity(nc, identity[:])


        persons = []
        for c in range(CHUNKS):
            rows = table[c * CHUNK_ROWS : (c + 1) * CHUNK_ROWS, :]
            chunk = held.tile([P, CHUNK_BLOCKS, P], BF16, name=f"persons{c}")
            if c < PAIRED_CHUNKS:
                nc.sync.dma_start(chunk[:], rows.rearrange("(p b) k -> p b k", p=P))
            else:
                nc.sync.dma_start(chunk[:], rows.rearrange("(b p) k -> p b k", p=P))
            persons.append(chunk)
        offsets = held.tile([P, N // 16], U16, name="offsets")
        nc.sync.dma_start(offsets[:], offs)
        wp1_sb = held.tile([P, EMBED], BF16, name="wp1_sb")
        nc.sync.dma_start(wp1_sb[:], wp1)
        bp1_sb = load_columns(nc, nc.sync, held, "bp1_sb", bp1)

        wp2_sb = held.tile([P, HALVES, EMBED], BF16, name="wp2_sb")
        nc.sync.dma_start(wp2_sb[:], wp2.rearrange("(e p) d -> p e d", p=P))
        bp2_sb = load_columns(nc, nc.sync, held, "bp2_sb", bp2)
        wf1_sb = held.tile([P, HALVES + 1, P], BF16, name="wf1_sb")
        nc.sync.dma_start(wf1_sb[:], wf1.rearrange("(r p) f -> p r f", p=P))
        bf1_sb = load_columns(nc, nc.sync, held, "bf1_sb", bf1)

        wt1_sb = load_columns(nc, nc.sync, held, "wt1_sb", wt1)
        bt1_sb = load_columns(nc, nc.sync, held, "bt1_sb", bt1)

        times = held.tile([P, N], F32, name="times")
        nc.sync.dma_start(times[:], t[0, :].partition_broadcast(P))

        zero = held.tile([P, 1], F32, name="zero")
        nc.vector.memset(zero[:], 0.0)
        unused = held.tile([P, 1], F32, name="unused")
        nc.scalar.activation(unused[:], zero[:], RELU)

        window_tile = shared.tile([P, N], BF16, tag="window_then_te", name="window_tile")
        window = window_tile[:, :PERSONS]
        with tc.psum_pool(name="flip", bufs=1) as flip:
            unread_ps = flip.tile([P, P], F32, name="unread_ps")
            for i in range(WARMING_MATMULS):
                nc.tensor.matmul(unread_ps[:], zeros[:], zeros[:], start=True, stop=True)

            for c in range(CHUNKS):
                flipped = flip.tile([P, CHUNK_BLOCKS, P], BF16, name=f"flipped{c}")
                for b in range(CHUNK_BLOCKS):
                    nc.tensor.transpose(flipped[:, b, :], persons[c][:, b, :], identity[:])
                window_chunk = window[:, c * CHUNK_ROWS : (c + 1) * CHUNK_ROWS]
                if c < PAIRED_CHUNKS:
                    nc.vector.tensor_copy(
                        window_chunk.rearrange("k (p b) -> k p b", p=P), flipped[:].rearrange("k b p -> k p b")
                    )
                else:
                    nc.vector.tensor_copy(window_chunk, flipped[:].rearrange("k b p -> k (b p)"))

        a_sb = held.tile([P, HALVES, N], BF16, name="a_sb")
        pe_sb = held.tile([P, HALVES, N], BF16, name="pe_sb")
        out_sb = held.tile([P, N], F32, name="out_sb")

        with tc.psum_pool(name="banks", bufs=8) as banks:
            for j in range(PIECES):
                for h in range(HALVES):
                    a_ps = banks.tile([P, PIECE], F32, tag="bank")
                    picked = window.indirect(offsets[:, j * LIST_COLUMNS : (j + 1) * LIST_COLUMNS])
                    nc.tensor.matmul(a_ps[:], wp1_sb[:, block_columns(h)], picked, start=True, stop=True)
                    add_bias(nc, h, a_sb[:, h, piece_columns(j)], a_ps[:], bp1_sb[:, h : h + 1], relu=True)

            te_sb = shared.tile([P, N], BF16, tag="window_then_te", name="te_sb")
            for j in range(PIECES):
                nc.scalar.activation(
                    te_sb[:, piece_columns(j)], times[:, piece_columns(j)], RELU, bias=bt1_sb[:], scale=wt1_sb[:]
                )

            def second_layer(j):
                for d in range(HALVES):
                    pe_ps = banks.tile([P, PIECE], F32, tag="bank")
                    for e in range(HALVES):
                        nc.tensor.matmul(
                            pe_ps[:],
                            wp2_sb[:, e, block_columns(d)],
                            a_sb[:, e, piece_columns(j)],
                            start=(e == 0),
                            stop=(e == HALVES - 1),
                        )
                    add_bias(nc, d, pe_sb[:, d, piece_columns(j)], pe_ps[:], bp2_sb[:, d : d + 1], relu=False)

            def flow_layer(j):
                for side in range(2):
                    first = j * PIECE + side * HALF_PIECE
                    columns = slice(first, first + HALF_PIECE)
                    out_ps = banks.tile([P, HALF_PIECE], F32, tag="bank")
                    nc.tensor.matmul(out_ps[:], wf1_sb[:, HALVES, :], te_sb[:, columns], start=True, stop=False)
                    for d in range(HALVES):
                        nc.tensor.matmul(
                            out_ps[:], wf1_sb[:, d, :], pe_sb[:, d, columns], start=False, stop=(d == HALVES - 1)
                        )
                    add_bias(nc, side, out_sb[:, columns], out_ps[:], bf1_sb[:], relu=True)
                    nc.sync.dma_start(out[:, columns], out_sb[:, columns])

            second_layer(0)
            for j in range(1, PIECES):
                second_layer(j)
                flow_layer(j - 1)
            flow_layer(PIECES - 1)
